import numpy as np
import ml_dtypes


def mxq(x, axis, fmt="e4m3"):
    dtype, down = {"e4m3": (ml_dtypes.float8_e4m3fn, 7), "e5m2": (ml_dtypes.float8_e5m2, 14)}[fmt]
    v = np.moveaxis(np.asarray(x, np.float32).astype(ml_dtypes.bfloat16).astype(np.float64), axis, -1)
    blocks = v.reshape(v.shape[:-1] + (-1, 32))
    amax = np.abs(blocks).max(-1, keepdims=True)
    byte = np.maximum(np.where(amax > 0, np.frexp(amax)[1] - 1 + 127, 0) - down, 1)
    scale = np.exp2(byte - 127.0)
    codes = (blocks / scale).astype(np.float32).astype(dtype).astype(np.float64)
    return np.moveaxis((codes * scale).reshape(v.shape), -1, axis)


WIDE = False


def mx_kscale(k):
    if not WIDE:
        return np.ones(k)
    levels = np.array([18, -18])
    if k % 512:
        return np.exp2(np.random.permutation(np.resize(levels, k // 32))).repeat(32)
    a = np.empty((k // 512, 16))
    for p in range(k // 512):
        a[p, :8] = np.random.permutation(np.resize(levels, 8))
        for g in range(8):
            far = levels[np.abs(levels - a[p, g]) >= 10]
            a[p, g + 8] = far[np.random.randint(len(far))]
    return np.exp2(a.ravel()).repeat(32)


BF16 = ml_dtypes.bfloat16


def bf(x):
    return np.asarray(x, np.float32).astype(BF16)


def f64(x):
    return np.asarray(x).astype(np.float64)


N, C, T, V, H, QK = 1, 128, 1024, 16, 2, 32
K = QK * V
MQ = np.sqrt(0.5 * np.sqrt(QK))


def frames(a):
    return np.swapaxes(a, 2, 3).reshape(N, H, T, K)


def unframes(a):
    return np.swapaxes(a.reshape(N, H, T, QK, V), 2, 3)


def scores(q, k):
    return frames(f64(q)) @ np.swapaxes(frames(f64(k)), 2, 3)


def setup_inputs():
    s = mx_kscale(T)[:, None]
    u = mx_kscale(T)
    q0 = bf(MQ * np.random.standard_normal((N, H, QK, T, 1)) + 1.6 * np.random.standard_normal((N, H, QK, T, V)))
    k0 = bf(MQ * np.random.standard_normal((N, H, QK, T, 1)) + 1.6 * np.random.standard_normal((N, H, QK, T, V)))
    alphas = bf(0.2 * (1.0 + 0.3 * np.random.standard_normal((1, H, 1, 1))))
    att1s = bf(np.eye(T)[None, None] + 0.05 * np.random.standard_normal((1, H, T, T)))
    g = bf(256.0 * np.random.standard_normal((N, H, T, T)) * np.exp2(np.random.randint(-6, 1, (N, H, T, 1))) / s * u)
    sc = scores(q0, k0)
    return {"q": bf(f64(q0) * s), "k": bf(f64(k0) / u[:, None]), "alphas": alphas, "att1s": att1s,
            "sc": np.asarray(sc, np.float32), "grad_out": g}


def reference(q, k, alphas, att1s, sc, grad_out):
    th = np.tanh(f64(sc) / (QK * V))
    dsc = f64(grad_out) * f64(alphas) * (1.0 - th * th) / (QK * V)
    qf = frames(f64(q))
    kf = frames(f64(k))
    dq = mxq(dsc, 3, "e5m2") @ mxq(kf, 2, "e4m3")
    dk = np.swapaxes(mxq(dsc, 2, "e5m2"), 2, 3) @ mxq(qf, 2, "e4m3")
    return unframes(dq), unframes(dk)

@@ -1,0 +1,291 @@
+from contextlib import ExitStack
+
+import concourse.mybir as mybir
+from concourse.masks import make_identity
+
+H, C, T, V = 2, 32, 1024, 16
+P = 128
+PACK = 4
+HALF = P * PACK
+NG = T // HALF
+K = C * V
+
+FLOPS = 2 * 2 * H * T * T * K
+BYTES = 2 * (2 * H * C * T * V) + 4 * H * T * T + 2 * H * T * T + 2 * (4 * H * C * T * V)
+
+F32 = mybir.dt.float32
+BF16 = mybir.dt.bfloat16
+U32 = mybir.dt.uint32
+U8 = mybir.dt.uint8
+E4 = mybir.dt.float8_e4m3fn_x4
+E5 = mybir.dt.float8_e5m2_x4
+ALU = mybir.AluOpType
+ACT = mybir.ActivationFunctionType
+
+SC_BUFS = 4
+PIECES = {0: 4, 1: 2, 2: 2}
+
+
+def tile_model_pa_v_kernel(tc, q, k, alphas, att1s, sc, grad_out, out_0, out_1):
+    nc = tc.nc
+    with ExitStack() as ctx:
+        one = ctx.enter_context(tc.tile_pool(name="one", bufs=1))
+        sc_pool = ctx.enter_context(tc.tile_pool(name="sc_pool", bufs=SC_BUFS))
+        g_pool = ctx.enter_context(tc.tile_pool(name="g_pool", bufs=3))
+        th_pool = ctx.enter_context(tc.tile_pool(name="th_pool", bufs=3))
+        d_pool = ctx.enter_context(tc.tile_pool(name="d_pool", bufs=2))
+        c3_pool = ctx.enter_context(tc.tile_pool(name="c3_pool", bufs=4))
+        c2_pool = ctx.enter_context(tc.tile_pool(name="c2_pool", bufs=3))
+        st_pool = ctx.enter_context(tc.tile_pool(name="st_pool", bufs=3))
+        ps_qk = ctx.enter_context(tc.psum_pool(name="ps_qk", bufs=2))
+        ps_dt = ctx.enter_context(tc.psum_pool(name="ps_dt", bufs=2))
+        ps_mm = ctx.enter_context(tc.psum_pool(name="ps_mm", bufs=4))
+
+        warm = one.tile([P, 1], F32)
+        nc.gpsimd.memset(warm[:], 0.0)
+        alpha_sb = one.tile([P, H], BF16)
+        nc.sync.dma_start(out=alpha_sb[:], in_=alphas.rearrange("a h b c -> (a h b c)").partition_broadcast(P))
+        warm_out = one.tile([P, 1], F32)
+        nc.scalar.activation(warm_out[:], warm[:], ACT.Tanh)
+        ident = one.tile([P, P], F32)
+        make_identity(nc, ident[:])
+        c_pos = one.tile([P, H], F32)
+        c_neg = one.tile([P, H], F32)
+        nc.gpsimd.tensor_scalar_mul(c_pos[:], alpha_sb[:], 1.0 / K)
+        nc.gpsimd.tensor_scalar_mul(c_neg[:], alpha_sb[:], -1.0 / K)
+        ident_hgc = one.tile([P, P], F32)
+        for h in range(H):
+            nc.vector.tensor_copy(
+                out=ident_hgc[:, 64 * h : 64 * h + 64].rearrange("p (g c) -> p g c", g=NG),
+                in_=ident[:, 64 * h : 64 * h + 64].rearrange("p (c g) -> p g c", g=NG),
+            )
+
+        k_raw = one.tile([P, HALF * V], BF16, tag="k_raw_q_il", align_bytes=64)
+        q_raw = one.tile([P, HALF * V], BF16)
+        k_codes = one.tile([P, H * NG, K], U32, align_bytes=64)
+        k_scales = one.tile([P, H * NG, K], U8, align_bytes=64)
+        q_codes = one.tile([P, H * NG, K], U32, align_bytes=64)
+        q_scales = one.tile([P, H * NG, K], U8, align_bytes=64)
+
+        sc_t, g_t, th_t, d_t, il_t, dt_t = {}, {}, {}, {}, {}, {}
+        dc_t, ds_t, tc_t, ts_t = {}, {}, {}, {}
+
+        def split(s):
+            return s // 4, (s // 2) % 2, s % 2
+
+        def load_sc(s, pieces=1):
+            h, g, gu = split(s)
+            sc_tile = sc_pool.tile([P, PACK, HALF], F32)
+            src = sc[0, h, HALF * g : HALF * (g + 1), HALF * gu : HALF * (gu + 1)].rearrange("(p j) u -> p j u", j=PACK)
+            w = PACK // pieces
+            for i in range(pieces):
+                nc.sync.dma_start(out=sc_tile[:, w * i : w * (i + 1), :], in_=src[:, w * i : w * (i + 1), :])
+            sc_t[s] = sc_tile
+
+        def load_g(h, g, halves=False):
+            g_tile = g_pool.tile([P, PACK, T], BF16)
+            src = grad_out[0, h, HALF * g : HALF * (g + 1), :].rearrange("(p j) u -> p j u", j=PACK)
+            g_t[(h, g)] = (g_tile, src)
+            if not halves:
+                nc.sync.dma_start(out=g_tile[:], in_=src)
+
+        def load_g_half(h, g, gu):
+            g_tile, src = g_t[(h, g)]
+            cols = slice(HALF * gu, HALF * (gu + 1))
+            nc.sync.dma_start(out=g_tile[:, :, cols], in_=src[:, :, cols])
+
+        def load_qk(tile, src):
+            nc.sync.dma_start(out=tile[:], in_=src.rearrange("n h c (g u) v -> (n h c g) (u v)", g=NG))
+
+        def tanh(s, pieces=1):
+            th = th_pool.tile([P, PACK * HALF], F32)
+            w = PACK * HALF // pieces
+            sc_flat = sc_t[s][:].rearrange("p j u -> p (j u)")
+            for i in range(pieces):
+                cols = slice(w * i, w * (i + 1))
+                nc.scalar.activation(th[:, cols], sc_flat[:, cols], ACT.Tanh, scale=1.0 / K)
+            th_t[s] = th
+
+        def slope(s, pieces=1):
+            h = s // 4
+            th = th_t[s]
+            w = PACK * HALF // pieces
+            for i in range(pieces):
+                cols = slice(w * i, w * (i + 1))
+                nc.vector.scalar_tensor_tensor(th[:, cols], th[:, cols], c_neg[:, h : h + 1], th[:, cols], ALU.mult, ALU.mult)
+
+        def dsc(s):
+            h, g, gu = split(s)
+            d = d_pool.tile([P, PACK, HALF], BF16, align_bytes=64)
+            nc.vector.scalar_tensor_tensor(
+                d[:],
+                th_t[s][:].rearrange("p (j u) -> p j u", j=PACK),
+                c_pos[:, h : h + 1],
+                g_t[(h, g)][0][:, :, HALF * gu : HALF * (gu + 1)],
+                ALU.add,
+                ALU.mult,
+            )
+            d_t[s] = d
+
+        def interleave(s):
+            il = d_pool.tile([P, PACK, P, PACK], BF16, align_bytes=64)
+            nc.vector.tensor_copy(out=il[:], in_=d_t[s][:].rearrange("p j (i r) -> p r i j", r=PACK))
+            il_t[s] = il
+
+        def quant_t(s):
+            h, g, gu = split(s)
+            if g == 0:
+                dc_tile = c3_pool.tile([P, NG, HALF], U32, align_bytes=64)
+                ds_tile = c3_pool.tile([P, NG, HALF], U8, align_bytes=64)
+                dc_t[(h, gu)] = dc_tile
+                ds_t[(h, gu)] = ds_tile
+            nc.vector.quantize_mx(
+                out=dc_t[(h, gu)][:, g, :].bitcast(E5),
+                scales=ds_t[(h, gu)][:, g, :],
+                in_=il_t[s][:].rearrange("p r i j -> p (r i j)"),
+            )
+
+        def transposes(s):
+            words = d_t[s][:].rearrange("p j u -> p (j u)").bitcast(F32)
+            banks = []
+            for b in range(2):
+                dps = ps_dt.tile([P, 2, 2, P], F32)
+                for jj in range(2):
+                    for e in range(2):
+                        base = (2 * b + jj) * (HALF // 2)
+                        nc.tensor.transpose(dps[:, jj, e, :], words[:, base + e : base + HALF // 2 : 2], ident[:])
+                banks.append(dps)
+            return banks
+
+        def copy_t(s, banks):
+            dt = d_pool.tile([P, PACK * P * PACK], BF16, align_bytes=64)
+            dw = dt[:].bitcast(F32).rearrange("p (b j m e) -> p b j m e", b=2, j=2, e=2)
+            for b in range(2):
+                nc.scalar.copy(out=dw[:, b], in_=banks[b][:].rearrange("p j e m -> p j m e"))
+            dt_t[s] = dt
+
+        def quant_u(s):
+            h, g, gu = split(s)
+            if gu == 0:
+                tc_tile = c2_pool.tile([P, NG, HALF], U32, align_bytes=64)
+                ts_tile = c2_pool.tile([P, NG, HALF], U8, align_bytes=64)
+                tc_t[(h, g)] = tc_tile
+                ts_t[(h, g)] = ts_tile
+            nc.vector.quantize_mx(
+                out=tc_t[(h, g)][:, gu, :].bitcast(E5),
+                scales=ts_t[(h, g)][:, gu, :],
+                in_=dt_t[s][:],
+            )
+
+        qk_il = {}
+
+        def qk_bank(name, raw, vp, engine):
+            if name not in qk_il:
+                tag = "k_il" if name == "k" else "k_raw_q_il"
+                xil = one.tile([P, H * NG * C, V // 2, 2 * PACK], BF16, tag=tag, align_bytes=64)
+                qk_il[name] = xil
+            words = raw[:].bitcast(F32)
+            xps = ps_qk.tile([P, PACK, P], F32)
+            step = PACK * V // 2
+            for r in range(PACK):
+                first = r * (V // 2) + vp
+                nc.tensor.transpose(xps[:, r, :], words[:, first : first + step * (P - 1) + 1 : step], ident_hgc[:])
+            src = xps[:].bitcast(BF16).rearrange("p r (x e) -> p x e r", e=2)
+            dst = qk_il[name][:, :, vp, :].rearrange("p x (e r) -> p x e r", e=2)
+            if engine == "s":
+                nc.scalar.copy(out=dst, in_=src)
+            else:
+                nc.vector.tensor_copy(out=dst, in_=src)
+
+        def qk_quant(name, codes, scales, h):
+            flat = qk_il[name][:].rearrange("p x w e -> p (x w e)")
+            for i in range(NG * h, NG * (h + 1)):
+                nc.vector.quantize_mx(out=codes[:, i, :].bitcast(E4), scales=scales[:, i, :], in_=flat[:, 4 * K * i : 4 * K * (i + 1)])
+
+        def product(codes, scales, x_codes, x_scales, h, out, half, pattern):
+            st = st_pool.tile([P, C, PACK, V], F32)
+            for m in range(PACK):
+                mm = ps_mm.tile([P, K], F32)
+                cols = slice(P * m, P * (m + 1))
+                for x in range(NG):
+                    nc.tensor.matmul_mx(
+                        out=mm[:],
+                        lhsT=codes[:, x, cols].bitcast(E5),
+                        lhsT_scale=scales[:, x, cols],
+                        rhs=x_codes[:, NG * h + x, :].bitcast(E4),
+                        rhs_scale=x_scales[:, NG * h + x, :],
+                        start=(x == 0),
+                        stop=(x == NG - 1),
+                    )
+                src = mm[:].rearrange("p (c v) -> p c v", v=V)
+                if pattern[m] == "s":
+                    nc.scalar.copy(out=st[:, :, m, :], in_=src)
+                else:
+                    nc.vector.tensor_copy(out=st[:, :, m, :], in_=src)
+            nc.sync.dma_start(
+                out=out[0, h, :, HALF * half : HALF * (half + 1), :].rearrange("c (p j) v -> p c (j v)", j=PACK),
+                in_=st[:].rearrange("p c j v -> p c (j v)"),
+            )
+
+        def product_q(h, g, pattern):
+            product(tc_t[(h, g)], ts_t[(h, g)], k_codes, k_scales, h, out_0, g, pattern)
+
+        def product_k(h, gu, pattern):
+            product(dc_t[(h, gu)], ds_t[(h, gu)], q_codes, q_scales, h, out_1, gu, pattern)
+
+        ctx.enter_context(tc.manual_schedule())
+
+        load_sc(0, pieces=4)
+        tanh(0, pieces=PIECES[0])
+        load_g(0, 0, halves=True)
+        load_g_half(0, 0, 0)
+        load_sc(1, pieces=2)
+        load_g_half(0, 0, 1)
+        load_sc(2, pieces=2)
+        load_qk(k_raw, k)
+        load_g(0, 1)
+        load_sc(3)
+        load_sc(4)
+        load_qk(q_raw, q)
+        load_g(1, 0)
+
+        first = {2: [("k", 0, "s"), ("k", 6, "s")], 3: [("k", 3, "s"), ("k", 2, "s")], 4: [("q", 5, "s"), ("q", 0, "s"), ("q", 7, "s")], 5: [("Q", 0, 0, "ssss"), ("kz", 1)], 7: [("Q", 1, 0, "ssss")], 8: [("K", 1, 0, "vsvs")]}
+        before = {1: [("k", 1, "s")], 2: [("k", 5, "s")], 5: [("q", 4, "v"), ("q", 1, "s"), ("Q", 0, 1, "ssss")], 6: [("K", 0, 1, "vvss")], 7: [("K", 0, 0, "vsss"), ("qz", 1)], 8: [("K", 1, 1, "svsv"), ("Q", 1, 1, "ssvs")]}
+        after = {2: [("k", 7, "v")], 3: [("k", 4, "s")], 4: [("q", 6, "s"), ("kz", 0), ("q", 2, "s"), ("q", 3, "s")], 5: [("qz", 0)]}
+
+        def side(items):
+            for item in items:
+                if item[0] == "k":
+                    qk_bank("k", k_raw, item[1], item[2])
+                elif item[0] == "q":
+                    qk_bank("q", q_raw, item[1], item[2])
+                elif item[0] == "kz":
+                    qk_quant("k", k_codes, k_scales, item[1])
+                elif item[0] == "qz":
+                    qk_quant("q", q_codes, q_scales, item[1])
+                elif item[0] == "Q":
+                    product_q(item[1], item[2], item[3])
+                else:
+                    product_k(item[1], item[2], item[3])
+
+        for s in range(9):
+            side(first.get(s, []))
+            if s + 1 < 8:
+                tanh(s + 1, pieces=PIECES.get(s + 1, 1))
+                if s < 3:
+                    load_sc(s + 5)
+            if s == 3:
+                load_g(1, 1)
+            if s < 8:
+                slope(s, pieces=PIECES.get(s, 1))
+            if s >= 1:
+                quant_t(s - 1)
+            if s < 8:
+                dsc(s)
+            if s >= 1:
+                quant_u(s - 1)
+            side(before.get(s, []))
+            if s < 8:
+                interleave(s)
+                copy_t(s, transposes(s))
+            side(after.get(s, []))

@@ -24,6 +24,19 @@ ACT = mybir.ActivationFunctionType
 
 SC_BUFS = 4
 PIECES = {0: 4, 1: 2, 2: 2}
+ORDER = (
+    "Lsc0_0 Lsc0_1 Lsc0_2 Lsc0_3 Lg00 Lsc1_0 Lsc1_1 Lk Lg01 T0_0 Lsc2_0 T0_1 W0_0 Lsc2_1 T0_2 W0_1 Lsc3_0 T0_3 "
+    "W0_2 W0_3 Lg2 D0 Lq T1_0 Lsc4_0 T1_1 X0 I0 W1_1 C0 W1_0 Lg6 kx2 kx0 kc2s Lg4 D1 kx1 kx3 kc0s Lsc5_0 kx4 "
+    "T2_0 kx5 I1 X1 T2_1 W2_0 kx6 C1 Lsc6_0 kx7 W2_1 kc5s kc3v kc4s D2 T3_0 A0_0 X2 kc6s Lsc7_0 I2 kc1s qx0 "
+    "qx3 W3_0 kc7s qx2 qx1 C2 qx7 kz0 T4_0 qx6 D3 qc1s B0_0 X3 qc6s I3 qc2s qx5 qx4 C3 W4_0 qc0s qc3s kz1 qc7s "
+    "A0_1 qc5s D4 T5_0 B0_1 X4 qc4s I4 MQ001 C4 MQ000 W5_0 MQ002 EQ000s MQ012 EQ001s MQ003 EQ002s MQ010 EQ012s "
+    "A4 MQ011 EQ003s D5 EQ010s MQ013 EQ011s EQ013s T6_0 qz0 Ss0Q0 X5 Ss0Q1 I5 MK010 MK003 C5 qz1 MK000 EK003s "
+    "MK002 EK000v EK010s MK011 W6_0 EK002s MK013 EK011s MK001 EK013s MK012 EK001s D6 EK012s T7_0 Ss0K0 Ss0K1 "
+    "B4 X6 A5 B5 NK113 C6 I6 NK112 MQ103 MQ102 EQ103s W7_0 MQ100 EQ102s MQ101 EQ100s NK111 EQ101s NK110 A6 "
+    "Ss1Q0 D7 MK103 MK102 EK103s EK102s MK100 B6 MK101 I7 EK100s X7 EK101s Ss1K0 NQ112 A7 C7 NQ113 MK113 MK110 "
+    "B7 EK113s MK112 MK111 EK110v EK112s NQ110 MQ112 EK111v MQ110 EQ112s Ss1K1 NQ111 EQ110v MQ111 MQ113 EQ111v "
+    "EQ113s Ss1Q1"
+)
 
 
 def tile_model_pa_v_kernel(tc, q, k, alphas, att1s, sc, grad_out, out_0, out_1):
@@ -32,14 +45,13 @@ def tile_model_pa_v_kernel(tc, q, k, alphas, att1s, sc, grad_out, out_0, out_1):
         one = ctx.enter_context(tc.tile_pool(name="one", bufs=1))
         sc_pool = ctx.enter_context(tc.tile_pool(name="sc_pool", bufs=SC_BUFS))
         g_pool = ctx.enter_context(tc.tile_pool(name="g_pool", bufs=3))
-        th_pool = ctx.enter_context(tc.tile_pool(name="th_pool", bufs=3))
+        th_pool = ctx.enter_context(tc.tile_pool(name="th_pool", bufs=2))
         d_pool = ctx.enter_context(tc.tile_pool(name="d_pool", bufs=2))
         c3_pool = ctx.enter_context(tc.tile_pool(name="c3_pool", bufs=4))
         c2_pool = ctx.enter_context(tc.tile_pool(name="c2_pool", bufs=3))
-        st_pool = ctx.enter_context(tc.tile_pool(name="st_pool", bufs=3))
-        ps_qk = ctx.enter_context(tc.psum_pool(name="ps_qk", bufs=2))
+        st_pool = ctx.enter_context(tc.tile_pool(name="st_pool", bufs=2))
         ps_dt = ctx.enter_context(tc.psum_pool(name="ps_dt", bufs=2))
-        ps_mm = ctx.enter_context(tc.psum_pool(name="ps_mm", bufs=4))
+        ps_bank = ctx.enter_context(tc.psum_pool(name="ps_bank", bufs=6))
 
         warm = one.tile([P, 1], F32)
         nc.gpsimd.memset(warm[:], 0.0)
@@ -61,58 +73,55 @@ def tile_model_pa_v_kernel(tc, q, k, alphas, att1s, sc, grad_out, out_0, out_1):
             )
 
         k_raw = one.tile([P, HALF * V], BF16, tag="k_raw_q_il", align_bytes=64)
-        q_raw = one.tile([P, HALF * V], BF16)
+        q_raw = one.tile([P, HALF * V], BF16, tag="q_raw_k_out", align_bytes=64)
         k_codes = one.tile([P, H * NG, K], U32, align_bytes=64)
         k_scales = one.tile([P, H * NG, K], U8, align_bytes=64)
         q_codes = one.tile([P, H * NG, K], U32, align_bytes=64)
         q_scales = one.tile([P, H * NG, K], U8, align_bytes=64)
 
         sc_t, g_t, th_t, d_t, il_t, dt_t = {}, {}, {}, {}, {}, {}
-        dc_t, ds_t, tc_t, ts_t = {}, {}, {}, {}
+        dc_t, tc_t, dps_t = {}, {}, {}
 
         def split(s):
             return s // 4, (s // 2) % 2, s % 2
 
-        def load_sc(s, pieces=1):
+        def load_sc(s, i):
             h, g, gu = split(s)
-            sc_tile = sc_pool.tile([P, PACK, HALF], F32)
+            if i == 0:
+                sc_tile = sc_pool.tile([P, PACK, HALF], F32)
+                sc_t[s] = sc_tile
             src = sc[0, h, HALF * g : HALF * (g + 1), HALF * gu : HALF * (gu + 1)].rearrange("(p j) u -> p j u", j=PACK)
-            w = PACK // pieces
-            for i in range(pieces):
-                nc.sync.dma_start(out=sc_tile[:, w * i : w * (i + 1), :], in_=src[:, w * i : w * (i + 1), :])
-            sc_t[s] = sc_tile
+            w = PACK // PIECES.get(s, 1)
+            js = slice(w * i, w * (i + 1))
+            nc.sync.dma_start(out=sc_t[s][:, js, :], in_=src[:, js, :])
 
-        def load_g(h, g, halves=False):
-            g_tile = g_pool.tile([P, PACK, T], BF16)
+        def load_g(h, g, gu=None):
+            if not gu:
+                g_tile = g_pool.tile([P, PACK, T], BF16)
+                g_t[(h, g)] = g_tile
             src = grad_out[0, h, HALF * g : HALF * (g + 1), :].rearrange("(p j) u -> p j u", j=PACK)
-            g_t[(h, g)] = (g_tile, src)
-            if not halves:
-                nc.sync.dma_start(out=g_tile[:], in_=src)
-
-        def load_g_half(h, g, gu):
-            g_tile, src = g_t[(h, g)]
-            cols = slice(HALF * gu, HALF * (gu + 1))
-            nc.sync.dma_start(out=g_tile[:, :, cols], in_=src[:, :, cols])
+            us = slice(0, T) if gu is None else slice(HALF * gu, HALF * (gu + 1))
+            nc.sync.dma_start(out=g_t[(h, g)][:, :, us], in_=src[:, :, us])
 
         def load_qk(tile, src):
             nc.sync.dma_start(out=tile[:], in_=src.rearrange("n h c (g u) v -> (n h c g) (u v)", g=NG))
 
-        def tanh(s, pieces=1):
-            th = th_pool.tile([P, PACK * HALF], F32)
-            w = PACK * HALF // pieces
-            sc_flat = sc_t[s][:].rearrange("p j u -> p (j u)")
-            for i in range(pieces):
-                cols = slice(w * i, w * (i + 1))
-                nc.scalar.activation(th[:, cols], sc_flat[:, cols], ACT.Tanh, scale=1.0 / K)
-            th_t[s] = th
+        def piece(s, i):
+            w = PACK * HALF // PIECES.get(s, 1)
+            return slice(w * i, w * (i + 1))
 
-        def slope(s, pieces=1):
-            h = s // 4
+        def tanh(s, i):
+            if i == 0:
+                th = th_pool.tile([P, PACK * HALF], F32)
+                th_t[s] = th
+            cols = piece(s, i)
+            nc.scalar.activation(th_t[s][:, cols], sc_t[s][:].rearrange("p j u -> p (j u)")[:, cols], ACT.Tanh, scale=1.0 / K)
+
+        def slope(s, i):
             th = th_t[s]
-            w = PACK * HALF // pieces
-            for i in range(pieces):
-                cols = slice(w * i, w * (i + 1))
-                nc.vector.scalar_tensor_tensor(th[:, cols], th[:, cols], c_neg[:, h : h + 1], th[:, cols], ALU.mult, ALU.mult)
+            cols = piece(s, i)
+            h = s // 4
+            nc.vector.scalar_tensor_tensor(th[:, cols], th[:, cols], c_neg[:, h : h + 1], th[:, cols], ALU.mult, ALU.mult)
 
         def dsc(s):
             h, g, gu = split(s)
@@ -121,29 +130,53 @@ def tile_model_pa_v_kernel(tc, q, k, alphas, att1s, sc, grad_out, out_0, out_1):
                 d[:],
                 th_t[s][:].rearrange("p (j u) -> p j u", j=PACK),
                 c_pos[:, h : h + 1],
-                g_t[(h, g)][0][:, :, HALF * gu : HALF * (gu + 1)],
+                g_t[(h, g)][:, :, HALF * gu : HALF * (gu + 1)],
                 ALU.add,
                 ALU.mult,
             )
             d_t[s] = d
 
         def interleave(s):
-            il = d_pool.tile([P, PACK, P, PACK], BF16, align_bytes=64)
-            nc.vector.tensor_copy(out=il[:], in_=d_t[s][:].rearrange("p j (i r) -> p r i j", r=PACK))
-            il_t[s] = il
+            h, g, gu = split(s)
+            if h == 0:
+                if (0, g) not in il_t:
+                    il = d_pool.tile([P, 2 * PACK, NG, P // 2, PACK], BF16, align_bytes=64)
+                    il_t[(0, g)] = il
+                for half in range(2):
+                    rows = slice(PACK * half, PACK * (half + 1))
+                    nc.vector.tensor_copy(
+                        out=il_t[(0, g)][:, rows, gu].rearrange("p m i j -> p i m j"),
+                        in_=d_t[s][:].rearrange("p j (i m) -> p i m j", m=2 * PACK)[:, :, rows, :],
+                    )
+            else:
+                il = d_pool.tile([P, PACK, P, PACK], BF16, align_bytes=64)
+                nc.vector.tensor_copy(
+                    out=il[:].rearrange("p r i j -> p i r j"),
+                    in_=d_t[s][:].rearrange("p j (i r) -> p i r j", r=PACK),
+                )
+                il_t[s] = il
+
+        def codes_tile(pool, store, key):
+            dcode = pool.tile([P, T], U32, align_bytes=64)
+            dscale = pool.tile([P, T], U8, align_bytes=64)
+            store[key] = (dcode, dscale)
+
+        def quant(pair, cols, in_):
+            nc.vector.quantize_mx(out=pair[0][:, cols].bitcast(E5), scales=pair[1][:, cols], in_=in_)
+
+        def quant_t0(g):
+            codes_tile(c3_pool, dc_t, (0, g))
+            quant(dc_t[(0, g)], slice(0, T), il_t[(0, g)][:].rearrange("p m h i j -> p (m h i j)"))
+
+        def quant_u0(gu):
+            codes_tile(c2_pool, tc_t, (0, gu))
+            quant(tc_t[(0, gu)], slice(0, T), dt_t[(0, gu)][:])
 
         def quant_t(s):
             h, g, gu = split(s)
-            if g == 0:
-                dc_tile = c3_pool.tile([P, NG, HALF], U32, align_bytes=64)
-                ds_tile = c3_pool.tile([P, NG, HALF], U8, align_bytes=64)
-                dc_t[(h, gu)] = dc_tile
-                ds_t[(h, gu)] = ds_tile
-            nc.vector.quantize_mx(
-                out=dc_t[(h, gu)][:, g, :].bitcast(E5),
-                scales=ds_t[(h, gu)][:, g, :],
-                in_=il_t[s][:].rearrange("p r i j -> p (r i j)"),
-            )
+            if (1, gu) not in dc_t:
+                codes_tile(c3_pool, dc_t, (1, gu))
+            quant(dc_t[(1, gu)], slice(HALF * g, HALF * (g + 1)), il_t[s][:].rearrange("p r i j -> p (r i j)"))
 
         def transposes(s):
             words = d_t[s][:].rearrange("p j u -> p (j u)").bitcast(F32)
@@ -155,137 +188,154 @@ def tile_model_pa_v_kernel(tc, q, k, alphas, att1s, sc, grad_out, out_0, out_1):
                         base = (2 * b + jj) * (HALF // 2)
                         nc.tensor.transpose(dps[:, jj, e, :], words[:, base + e : base + HALF // 2 : 2], ident[:])
                 banks.append(dps)
-            return banks
+            dps_t[s] = banks
 
-        def copy_t(s, banks):
-            dt = d_pool.tile([P, PACK * P * PACK], BF16, align_bytes=64)
-            dw = dt[:].bitcast(F32).rearrange("p (b j m e) -> p b j m e", b=2, j=2, e=2)
-            for b in range(2):
-                nc.scalar.copy(out=dw[:, b], in_=banks[b][:].rearrange("p j e m -> p j m e"))
-            dt_t[s] = dt
+        def copy_t(s):
+            h, g, gu = split(s)
+            banks = dps_t[s]
+            if h == 0:
+                if (0, gu) not in dt_t:
+                    dt = d_pool.tile([P, 2 * T * 2], BF16, align_bytes=64)
+                    dt_t[(0, gu)] = dt
+                dw = dt_t[(0, gu)][:].bitcast(F32).rearrange("p (a j h i e) -> p a j h i e", a=2, j=PACK, h=NG, e=2)
+                for j in range(PACK):
+                    nc.scalar.copy(out=dw[:, :, j, g], in_=banks[j // 2][:, j % 2].rearrange("p e (i a) -> p a i e", a=2))
+            else:
+                dt = d_pool.tile([P, PACK * P * PACK], BF16, align_bytes=64)
+                dw = dt[:].bitcast(F32).rearrange("p (b j m e) -> p b j m e", b=2, j=2, e=2)
+                for b in range(2):
+                    nc.scalar.copy(out=dw[:, b], in_=banks[b][:].rearrange("p j e m -> p j m e"))
+                dt_t[s] = dt
 
         def quant_u(s):
             h, g, gu = split(s)
-            if gu == 0:
-                tc_tile = c2_pool.tile([P, NG, HALF], U32, align_bytes=64)
-                ts_tile = c2_pool.tile([P, NG, HALF], U8, align_bytes=64)
-                tc_t[(h, g)] = tc_tile
-                ts_t[(h, g)] = ts_tile
-            nc.vector.quantize_mx(
-                out=tc_t[(h, g)][:, gu, :].bitcast(E5),
-                scales=ts_t[(h, g)][:, gu, :],
-                in_=dt_t[s][:],
-            )
+            if (1, g) not in tc_t:
+                codes_tile(c2_pool, tc_t, (1, g))
+            quant(tc_t[(1, g)], slice(HALF * gu, HALF * (gu + 1)), dt_t[s][:])
 
-        qk_il = {}
+        qk_il, qk_ps = {}, {}
 
-        def qk_bank(name, raw, vp, engine):
-            if name not in qk_il:
-                tag = "k_il" if name == "k" else "k_raw_q_il"
-                xil = one.tile([P, H * NG * C, V // 2, 2 * PACK], BF16, tag=tag, align_bytes=64)
-                qk_il[name] = xil
-            words = raw[:].bitcast(F32)
-            xps = ps_qk.tile([P, PACK, P], F32)
+        def copy_out(engine, out, in_):
+            if engine == "s":
+                nc.scalar.copy(out=out, in_=in_)
+            else:
+                nc.vector.tensor_copy(out=out, in_=in_)
+
+        def qk_transpose(name, vp):
+            words = (k_raw if name == "k" else q_raw)[:].bitcast(F32)
+            xps = ps_bank.tile([P, PACK, P], F32, tag="bank")
             step = PACK * V // 2
             for r in range(PACK):
                 first = r * (V // 2) + vp
                 nc.tensor.transpose(xps[:, r, :], words[:, first : first + step * (P - 1) + 1 : step], ident_hgc[:])
-            src = xps[:].bitcast(BF16).rearrange("p r (x e) -> p x e r", e=2)
-            dst = qk_il[name][:, :, vp, :].rearrange("p x (e r) -> p x e r", e=2)
-            if engine == "s":
-                nc.scalar.copy(out=dst, in_=src)
-            else:
-                nc.vector.tensor_copy(out=dst, in_=src)
+            qk_ps[(name, vp)] = xps
+
+        def qk_copy(name, vp, engine):
+            if name not in qk_il:
+                tag = "k_il_q_out" if name == "k" else "k_raw_q_il"
+                xil = one.tile([P, H * NG * C, V // 2, 2 * PACK], BF16, tag=tag, align_bytes=64)
+                qk_il[name] = xil
+            copy_out(
+                engine,
+                qk_il[name][:, :, vp, :].rearrange("p x (e r) -> p x e r", e=2),
+                qk_ps[(name, vp)][:].bitcast(BF16).rearrange("p r (x e) -> p x e r", e=2),
+            )
 
         def qk_quant(name, codes, scales, h):
             flat = qk_il[name][:].rearrange("p x w e -> p (x w e)")
             for i in range(NG * h, NG * (h + 1)):
                 nc.vector.quantize_mx(out=codes[:, i, :].bitcast(E4), scales=scales[:, i, :], in_=flat[:, 4 * K * i : 4 * K * (i + 1)])
 
-        def product(codes, scales, x_codes, x_scales, h, out, half, pattern):
-            st = st_pool.tile([P, C, PACK, V], F32)
-            for m in range(PACK):
-                mm = ps_mm.tile([P, K], F32)
-                cols = slice(P * m, P * (m + 1))
-                for x in range(NG):
-                    nc.tensor.matmul_mx(
-                        out=mm[:],
-                        lhsT=codes[:, x, cols].bitcast(E5),
-                        lhsT_scale=scales[:, x, cols],
-                        rhs=x_codes[:, NG * h + x, :].bitcast(E4),
-                        rhs_scale=x_scales[:, NG * h + x, :],
-                        start=(x == 0),
-                        stop=(x == NG - 1),
-                    )
-                src = mm[:].rearrange("p (c v) -> p c v", v=V)
-                if pattern[m] == "s":
-                    nc.scalar.copy(out=st[:, :, m, :], in_=src)
+        st_t, mm_t = {}, {}
+
+        def multiply(name, h, half, m, passes):
+            codes = tc_t if name == "Q" else dc_t
+            x_codes, x_scales = (k_codes, k_scales) if name == "Q" else (q_codes, q_scales)
+            if passes[0] == 0:
+                mm = ps_bank.tile([P, K], F32, tag="bank")
+                mm_t[(name, h, half, m)] = mm
+            for x in passes:
+                if h == 0:
+                    lhs, first = codes[(0, x)], P * (PACK * half + m)
                 else:
-                    nc.vector.tensor_copy(out=st[:, :, m, :], in_=src)
-            nc.sync.dma_start(
-                out=out[0, h, :, HALF * half : HALF * (half + 1), :].rearrange("c (p j) v -> p c (j v)", j=PACK),
-                in_=st[:].rearrange("p c j v -> p c (j v)"),
-            )
+                    lhs, first = codes[(1, half)], HALF * x + P * m
+                nc.tensor.matmul_mx(
+                    out=mm_t[(name, h, half, m)][:],
+                    lhsT=lhs[0][:, first : first + P].bitcast(E5),
+                    lhsT_scale=lhs[1][:, first : first + P],
+                    rhs=x_codes[:, NG * h + x, :].bitcast(E4),
+                    rhs_scale=x_scales[:, NG * h + x, :],
+                    start=(x == 0),
+                    stop=(x == NG - 1),
+                )
 
-        def product_q(h, g, pattern):
-            product(tc_t[(h, g)], ts_t[(h, g)], k_codes, k_scales, h, out_0, g, pattern)
+        def evacuate(name, h, half, m, engine):
+            key = (name, 0) if h == 0 else (name, 1, half)
+            if key not in st_t:
+                if h == 0:
+                    st = one.tile([P, C, 2 * PACK, V], F32, tag="k_il_q_out" if name == "Q" else "q_raw_k_out", align_bytes=64)
+                elif half == 0:
+                    st = st_pool.tile([P, C, PACK, V], F32, align_bytes=64)
+                else:
+                    st = one.tile([P, C, PACK, V], F32, tag="k_il_q_out" if name == "Q" else "k_raw_q_il", align_bytes=64)
+                st_t[key] = st
+            row = PACK * half + m if h == 0 else m
+            copy_out(engine, st_t[key][:, :, row, :], mm_t[(name, h, half, m)][:].rearrange("p (c v) -> p c v", v=V))
 
-        def product_k(h, gu, pattern):
-            product(dc_t[(h, gu)], ds_t[(h, gu)], q_codes, q_scales, h, out_1, gu, pattern)
+        def store(name, h, part):
+            out = out_0 if name == "Q" else out_1
+            if h == 0:
+                cs = slice(C // 2 * part, C // 2 * (part + 1))
+                dst, src, runs = out[0, 0, cs], st_t[(name, 0)][:, cs], 2 * PACK
+            else:
+                dst, src, runs = out[0, 1, :, HALF * part : HALF * (part + 1), :], st_t[(name, 1, part)][:], PACK
+            nc.sync.dma_start(out=dst.rearrange("c (p m) v -> p c (m v)", m=runs), in_=src.rearrange("p c m v -> p c (m v)"))
 
         ctx.enter_context(tc.manual_schedule())
-
-        load_sc(0, pieces=4)
-        tanh(0, pieces=PIECES[0])
-        load_g(0, 0, halves=True)
-        load_g_half(0, 0, 0)
-        load_sc(1, pieces=2)
-        load_g_half(0, 0, 1)
-        load_sc(2, pieces=2)
-        load_qk(k_raw, k)
-        load_g(0, 1)
-        load_sc(3)
-        load_sc(4)
-        load_qk(q_raw, q)
-        load_g(1, 0)
-
-        first = {2: [("k", 0, "s"), ("k", 6, "s")], 3: [("k", 3, "s"), ("k", 2, "s")], 4: [("q", 5, "s"), ("q", 0, "s"), ("q", 7, "s")], 5: [("Q", 0, 0, "ssss"), ("kz", 1)], 7: [("Q", 1, 0, "ssss")], 8: [("K", 1, 0, "vsvs")]}
-        before = {1: [("k", 1, "s")], 2: [("k", 5, "s")], 5: [("q", 4, "v"), ("q", 1, "s"), ("Q", 0, 1, "ssss")], 6: [("K", 0, 1, "vvss")], 7: [("K", 0, 0, "vsss"), ("qz", 1)], 8: [("K", 1, 1, "svsv"), ("Q", 1, 1, "ssvs")]}
-        after = {2: [("k", 7, "v")], 3: [("k", 4, "s")], 4: [("q", 6, "s"), ("kz", 0), ("q", 2, "s"), ("q", 3, "s")], 5: [("qz", 0)]}
-
-        def side(items):
-            for item in items:
-                if item[0] == "k":
-                    qk_bank("k", k_raw, item[1], item[2])
-                elif item[0] == "q":
-                    qk_bank("q", q_raw, item[1], item[2])
-                elif item[0] == "kz":
-                    qk_quant("k", k_codes, k_scales, item[1])
-                elif item[0] == "qz":
-                    qk_quant("q", q_codes, q_scales, item[1])
-                elif item[0] == "Q":
-                    product_q(item[1], item[2], item[3])
+        for op in ORDER.split():
+            name, args = op[0], op[1:]
+            if name == "L":
+                if args == "k":
+                    load_qk(k_raw, k)
+                elif args == "q":
+                    load_qk(q_raw, q)
+                elif args[0] == "s":
+                    load_sc(int(args[2]), int(args[4]))
+                elif args in ("g00", "g01"):
+                    load_g(0, 0, int(args[2]))
                 else:
-                    product_k(item[1], item[2], item[3])
-
-        for s in range(9):
-            side(first.get(s, []))
-            if s + 1 < 8:
-                tanh(s + 1, pieces=PIECES.get(s + 1, 1))
-                if s < 3:
-                    load_sc(s + 5)
-            if s == 3:
-                load_g(1, 1)
-            if s < 8:
-                slope(s, pieces=PIECES.get(s, 1))
-            if s >= 1:
-                quant_t(s - 1)
-            if s < 8:
-                dsc(s)
-            if s >= 1:
-                quant_u(s - 1)
-            side(before.get(s, []))
-            if s < 8:
-                interleave(s)
-                copy_t(s, transposes(s))
-            side(after.get(s, []))
+                    load_g(int(args[1]) // 4, int(args[1]) // 2 % 2)
+            elif name in "kq" and args[0] == "x":
+                qk_transpose(name, int(args[1]))
+            elif name in "kq" and args[0] == "c":
+                qk_copy(name, int(args[1]), args[2])
+            elif name in "kq":
+                qk_quant(name, k_codes if name == "k" else q_codes, k_scales if name == "k" else q_scales, int(args[1]))
+            elif name == "T":
+                tanh(int(args[0]), int(args[2]))
+            elif name == "W":
+                slope(int(args[0]), int(args[2]))
+            elif name == "D":
+                dsc(int(args))
+            elif name == "I":
+                interleave(int(args))
+            elif name == "X":
+                transposes(int(args))
+            elif name == "C":
+                copy_t(int(args))
+            elif name == "A" and args[1:2] == "_":
+                quant_t0(int(args[2]))
+            elif name == "B" and args[1:2] == "_":
+                quant_u0(int(args[2]))
+            elif name == "A":
+                quant_t(int(args))
+            elif name == "B":
+                quant_u(int(args))
+            elif name == "N":
+                multiply(args[0], int(args[1]), int(args[2]), int(args[3]), [0])
+            elif name == "M":
+                multiply(args[0], int(args[1]), int(args[2]), int(args[3]), [1] if args[1:3] == "11" else [0, 1])
+            elif name == "E":
+                evacuate(args[0], int(args[1]), int(args[2]), int(args[3]), args[4])
+            elif name == "S":
+                store(args[2], int(args[1]), int(args[3]))

@@ -9,6 +9,7 @@ PACK = 4
 HALF = P * PACK
 NG = T // HALF
 K = C * V
+PAIRS = V // 2
 
 FLOPS = 2 * 2 * H * T * T * K
 BYTES = 2 * (2 * H * C * T * V) + 4 * H * T * T + 2 * H * T * T + 2 * (4 * H * C * T * V)
@@ -22,20 +23,23 @@ E5 = mybir.dt.float8_e5m2_x4
 ALU = mybir.AluOpType
 ACT = mybir.ActivationFunctionType
 
-SC_BUFS = 4
-PIECES = {0: 4, 1: 2, 2: 2}
+PIECES = {0: 4, 1: 2, 2: 2, 4: 2, 6: 2}
+
+AHEAD = 2
+
+LOADS = (
+    "sc:0:0 g:0:0 sc:0:1 g:0:1 sc:1 x:k g:1 x:q sc:2 g:2 sc:3 g:3"
+)
+
 ORDER = (
-    "Lsc0_0 Lsc0_1 Lsc0_2 Lsc0_3 Lg00 Lsc1_0 Lsc1_1 Lk Lg01 T0_0 Lsc2_0 T0_1 W0_0 Lsc2_1 T0_2 W0_1 Lsc3_0 T0_3 "
-    "W0_2 W0_3 Lg2 D0 Lq T1_0 Lsc4_0 T1_1 X0 I0 W1_1 C0 W1_0 Lg6 kx2 kx0 kc2s Lg4 D1 kx1 kx3 kc0s Lsc5_0 kx4 "
-    "T2_0 kx5 I1 X1 T2_1 W2_0 kx6 C1 Lsc6_0 kx7 W2_1 kc5s kc3v kc4s D2 T3_0 A0_0 X2 kc6s Lsc7_0 I2 kc1s qx0 "
-    "qx3 W3_0 kc7s qx2 qx1 C2 qx7 kz0 T4_0 qx6 D3 qc1s B0_0 X3 qc6s I3 qc2s qx5 qx4 C3 W4_0 qc0s qc3s kz1 qc7s "
-    "A0_1 qc5s D4 T5_0 B0_1 X4 qc4s I4 MQ001 C4 MQ000 W5_0 MQ002 EQ000s MQ012 EQ001s MQ003 EQ002s MQ010 EQ012s "
-    "A4 MQ011 EQ003s D5 EQ010s MQ013 EQ011s EQ013s T6_0 qz0 Ss0Q0 X5 Ss0Q1 I5 MK010 MK003 C5 qz1 MK000 EK003s "
-    "MK002 EK000v EK010s MK011 W6_0 EK002s MK013 EK011s MK001 EK013s MK012 EK001s D6 EK012s T7_0 Ss0K0 Ss0K1 "
-    "B4 X6 A5 B5 NK113 C6 I6 NK112 MQ103 MQ102 EQ103s W7_0 MQ100 EQ102s MQ101 EQ100s NK111 EQ101s NK110 A6 "
-    "Ss1Q0 D7 MK103 MK102 EK103s EK102s MK100 B6 MK101 I7 EK100s X7 EK101s Ss1K0 NQ112 A7 C7 NQ113 MK113 MK110 "
-    "B7 EK113s MK112 MK111 EK110v EK112s NQ110 MQ112 EK111v MQ110 EQ112s Ss1K1 NQ111 EQ110v MQ111 MQ113 EQ111v "
-    "EQ113s Ss1Q1"
+    "tanh:0 slope:0 dsc:0 tanh:1 turn:0 slope:1 tanh:2 mix:0 dsc:1 slope:2 tanh:3 turn:1 mix:1 turnx:k:0:s "
+    "turnx:k:1:s slope:3 turnx:k:2:s turnx:k:3:s qt:0:0 dsc:2 turnx:k:4:s turnx:k:5:s turnx:k:6:s turn:2 "
+    "turnx:q:0:s dsc:3 mix:2 mix:3 turnx:k:7:v turnx:q:1:s turnx:q:2:s turn:3 qt:0:1 qx:k:1 turnx:q:3:s qx:k:0 "
+    "tanh:4 turnx:q:4:s qu:0:0 qu:0:1 turnx:q:5:s turnx:q:6:v product:k:0:0:ssss product:k:0:1:ssss slope:4 "
+    "turnx:q:7:v dsc:4 tanh:5 qx:q:0 mix:4 tanh:6 turn:4 qx:q:1 slope:5 product:q:0:0:ssss slope:6 "
+    "product:q:0:1:ssss dsc:5 turn:5 dsc:6 tanh:7 qt:1:0 qu:1:0 qu:1:1 mix:6 product:k:1:0:ssss slope:7 qt:1:2 "
+    "turn:6 product:q:1:0:ssss mix:5 dsc:7 qt:1:1 turn:7 mix:7 open:q:1:1 qt:1:3 qu:1:2 qu:1:3 "
+    "product:q:1:1:vsvsvvss product:k:1:1:vvvvssss"
 )
 
 
@@ -43,22 +47,22 @@ def tile_model_pa_v_kernel(tc, q, k, alphas, att1s, sc, grad_out, out_0, out_1):
     nc = tc.nc
     with ExitStack() as ctx:
         one = ctx.enter_context(tc.tile_pool(name="one", bufs=1))
-        sc_pool = ctx.enter_context(tc.tile_pool(name="sc_pool", bufs=SC_BUFS))
+        sc_pool = ctx.enter_context(tc.tile_pool(name="sc_pool", bufs=2))
         g_pool = ctx.enter_context(tc.tile_pool(name="g_pool", bufs=3))
         th_pool = ctx.enter_context(tc.tile_pool(name="th_pool", bufs=2))
         d_pool = ctx.enter_context(tc.tile_pool(name="d_pool", bufs=2))
-        c3_pool = ctx.enter_context(tc.tile_pool(name="c3_pool", bufs=4))
-        c2_pool = ctx.enter_context(tc.tile_pool(name="c2_pool", bufs=3))
+        t_code_pool = ctx.enter_context(tc.tile_pool(name="t_code_pool", bufs=4))
+        u_code_pool = ctx.enter_context(tc.tile_pool(name="u_code_pool", bufs=3))
         st_pool = ctx.enter_context(tc.tile_pool(name="st_pool", bufs=2))
-        ps_dt = ctx.enter_context(tc.psum_pool(name="ps_dt", bufs=2))
+        ps_d = ctx.enter_context(tc.psum_pool(name="ps_d", bufs=2))
         ps_bank = ctx.enter_context(tc.psum_pool(name="ps_bank", bufs=6))
 
-        warm = one.tile([P, 1], F32)
-        nc.gpsimd.memset(warm[:], 0.0)
+        warm_in = one.tile([P, 1], F32)
+        nc.gpsimd.memset(warm_in[:], 0.0)
         alpha_sb = one.tile([P, H], BF16)
         nc.sync.dma_start(out=alpha_sb[:], in_=alphas.rearrange("a h b c -> (a h b c)").partition_broadcast(P))
         warm_out = one.tile([P, 1], F32)
-        nc.scalar.activation(warm_out[:], warm[:], ACT.Tanh)
+        nc.scalar.activation(warm_out[:], warm_in[:], ACT.Tanh)
         ident = one.tile([P, P], F32)
         make_identity(nc, ident[:])
         c_pos = one.tile([P, H], F32)
@@ -67,153 +71,32 @@ def tile_model_pa_v_kernel(tc, q, k, alphas, att1s, sc, grad_out, out_0, out_1):
         nc.gpsimd.tensor_scalar_mul(c_neg[:], alpha_sb[:], -1.0 / K)
         ident_hgc = one.tile([P, P], F32)
         for h in range(H):
+            cols = slice(C * NG * h, C * NG * (h + 1))
             nc.vector.tensor_copy(
-                out=ident_hgc[:, 64 * h : 64 * h + 64].rearrange("p (g c) -> p g c", g=NG),
-                in_=ident[:, 64 * h : 64 * h + 64].rearrange("p (c g) -> p g c", g=NG),
+                out=ident_hgc[:, cols].rearrange("p (g c) -> p g c", g=NG),
+                in_=ident[:, cols].rearrange("p (c g) -> p g c", g=NG),
             )
 
-        k_raw = one.tile([P, HALF * V], BF16, tag="k_raw_q_il", align_bytes=64)
-        q_raw = one.tile([P, HALF * V], BF16, tag="q_raw_k_out", align_bytes=64)
-        k_codes = one.tile([P, H * NG, K], U32, align_bytes=64)
-        k_scales = one.tile([P, H * NG, K], U8, align_bytes=64)
-        q_codes = one.tile([P, H * NG, K], U32, align_bytes=64)
-        q_scales = one.tile([P, H * NG, K], U8, align_bytes=64)
+        tag_a, tag_b, tag_c = "k_raw_q_mix", "k_mix_q_out", "q_raw_k_out"
+        raw = {}
+        k_raw = one.tile([P, HALF * V], BF16, tag=tag_a, align_bytes=64)
+        q_raw = one.tile([P, HALF * V], BF16, tag=tag_c, align_bytes=64)
+        raw["k"], raw["q"] = (k_raw, k), (q_raw, q)
+        x_codes = {}
+        for name in "kq":
+            codes = one.tile([P, H * NG, K], U32, name=name + "_codes", align_bytes=64)
+            scales = one.tile([P, H * NG, K], U8, name=name + "_scales", align_bytes=64)
+            x_codes[name] = (codes, scales)
 
-        sc_t, g_t, th_t, d_t, il_t, dt_t = {}, {}, {}, {}, {}, {}
-        dc_t, tc_t, dps_t = {}, {}, {}
+        sc_t, g_t, th_t, d_t, d_ps, mix_t, turned_t = {}, {}, {}, {}, {}, {}, {}
+        t_codes, u_codes, x_ps, x_mix, mm_t, st_t = {}, {}, {}, {}, {}, {}
 
         def split(s):
             return s // 4, (s // 2) % 2, s % 2
 
-        def load_sc(s, i):
-            h, g, gu = split(s)
-            if i == 0:
-                sc_tile = sc_pool.tile([P, PACK, HALF], F32)
-                sc_t[s] = sc_tile
-            src = sc[0, h, HALF * g : HALF * (g + 1), HALF * gu : HALF * (gu + 1)].rearrange("(p j) u -> p j u", j=PACK)
-            w = PACK // PIECES.get(s, 1)
-            js = slice(w * i, w * (i + 1))
-            nc.sync.dma_start(out=sc_t[s][:, js, :], in_=src[:, js, :])
-
-        def load_g(h, g, gu=None):
-            if not gu:
-                g_tile = g_pool.tile([P, PACK, T], BF16)
-                g_t[(h, g)] = g_tile
-            src = grad_out[0, h, HALF * g : HALF * (g + 1), :].rearrange("(p j) u -> p j u", j=PACK)
-            us = slice(0, T) if gu is None else slice(HALF * gu, HALF * (gu + 1))
-            nc.sync.dma_start(out=g_t[(h, g)][:, :, us], in_=src[:, :, us])
-
-        def load_qk(tile, src):
-            nc.sync.dma_start(out=tile[:], in_=src.rearrange("n h c (g u) v -> (n h c g) (u v)", g=NG))
-
         def piece(s, i):
-            w = PACK * HALF // PIECES.get(s, 1)
-            return slice(w * i, w * (i + 1))
-
-        def tanh(s, i):
-            if i == 0:
-                th = th_pool.tile([P, PACK * HALF], F32)
-                th_t[s] = th
-            cols = piece(s, i)
-            nc.scalar.activation(th_t[s][:, cols], sc_t[s][:].rearrange("p j u -> p (j u)")[:, cols], ACT.Tanh, scale=1.0 / K)
-
-        def slope(s, i):
-            th = th_t[s]
-            cols = piece(s, i)
-            h = s // 4
-            nc.vector.scalar_tensor_tensor(th[:, cols], th[:, cols], c_neg[:, h : h + 1], th[:, cols], ALU.mult, ALU.mult)
-
-        def dsc(s):
-            h, g, gu = split(s)
-            d = d_pool.tile([P, PACK, HALF], BF16, align_bytes=64)
-            nc.vector.scalar_tensor_tensor(
-                d[:],
-                th_t[s][:].rearrange("p (j u) -> p j u", j=PACK),
-                c_pos[:, h : h + 1],
-                g_t[(h, g)][:, :, HALF * gu : HALF * (gu + 1)],
-                ALU.add,
-                ALU.mult,
-            )
-            d_t[s] = d
-
-        def interleave(s):
-            h, g, gu = split(s)
-            if h == 0:
-                if (0, g) not in il_t:
-                    il = d_pool.tile([P, 2 * PACK, NG, P // 2, PACK], BF16, align_bytes=64)
-                    il_t[(0, g)] = il
-                for half in range(2):
-                    rows = slice(PACK * half, PACK * (half + 1))
-                    nc.vector.tensor_copy(
-                        out=il_t[(0, g)][:, rows, gu].rearrange("p m i j -> p i m j"),
-                        in_=d_t[s][:].rearrange("p j (i m) -> p i m j", m=2 * PACK)[:, :, rows, :],
-                    )
-            else:
-                il = d_pool.tile([P, PACK, P, PACK], BF16, align_bytes=64)
-                nc.vector.tensor_copy(
-                    out=il[:].rearrange("p r i j -> p i r j"),
-                    in_=d_t[s][:].rearrange("p j (i r) -> p i r j", r=PACK),
-                )
-                il_t[s] = il
-
-        def codes_tile(pool, store, key):
-            dcode = pool.tile([P, T], U32, align_bytes=64)
-            dscale = pool.tile([P, T], U8, align_bytes=64)
-            store[key] = (dcode, dscale)
-
-        def quant(pair, cols, in_):
-            nc.vector.quantize_mx(out=pair[0][:, cols].bitcast(E5), scales=pair[1][:, cols], in_=in_)
-
-        def quant_t0(g):
-            codes_tile(c3_pool, dc_t, (0, g))
-            quant(dc_t[(0, g)], slice(0, T), il_t[(0, g)][:].rearrange("p m h i j -> p (m h i j)"))
-
-        def quant_u0(gu):
-            codes_tile(c2_pool, tc_t, (0, gu))
-            quant(tc_t[(0, gu)], slice(0, T), dt_t[(0, gu)][:])
-
-        def quant_t(s):
-            h, g, gu = split(s)
-            if (1, gu) not in dc_t:
-                codes_tile(c3_pool, dc_t, (1, gu))
-            quant(dc_t[(1, gu)], slice(HALF * g, HALF * (g + 1)), il_t[s][:].rearrange("p r i j -> p (r i j)"))
-
-        def transposes(s):
-            words = d_t[s][:].rearrange("p j u -> p (j u)").bitcast(F32)
-            banks = []
-            for b in range(2):
-                dps = ps_dt.tile([P, 2, 2, P], F32)
-                for jj in range(2):
-                    for e in range(2):
-                        base = (2 * b + jj) * (HALF // 2)
-                        nc.tensor.transpose(dps[:, jj, e, :], words[:, base + e : base + HALF // 2 : 2], ident[:])
-                banks.append(dps)
-            dps_t[s] = banks
-
-        def copy_t(s):
-            h, g, gu = split(s)
-            banks = dps_t[s]
-            if h == 0:
-                if (0, gu) not in dt_t:
-                    dt = d_pool.tile([P, 2 * T * 2], BF16, align_bytes=64)
-                    dt_t[(0, gu)] = dt
-                dw = dt_t[(0, gu)][:].bitcast(F32).rearrange("p (a j h i e) -> p a j h i e", a=2, j=PACK, h=NG, e=2)
-                for j in range(PACK):
-                    nc.scalar.copy(out=dw[:, :, j, g], in_=banks[j // 2][:, j % 2].rearrange("p e (i a) -> p a i e", a=2))
-            else:
-                dt = d_pool.tile([P, PACK * P * PACK], BF16, align_bytes=64)
-                dw = dt[:].bitcast(F32).rearrange("p (b j m e) -> p b j m e", b=2, j=2, e=2)
-                for b in range(2):
-                    nc.scalar.copy(out=dw[:, b], in_=banks[b][:].rearrange("p j e m -> p j m e"))
-                dt_t[s] = dt
-
-        def quant_u(s):
-            h, g, gu = split(s)
-            if (1, g) not in tc_t:
-                codes_tile(c2_pool, tc_t, (1, g))
-            quant(tc_t[(1, g)], slice(HALF * gu, HALF * (gu + 1)), dt_t[s][:])
-
-        qk_il, qk_ps = {}, {}
+            width = PACK * HALF // PIECES.get(s, 1)
+            return slice(width * i, width * (i + 1))
 
         def copy_out(engine, out, in_):
             if engine == "s":
@@ -221,121 +104,239 @@ def tile_model_pa_v_kernel(tc, q, k, alphas, att1s, sc, grad_out, out_0, out_1):
             else:
                 nc.vector.tensor_copy(out=out, in_=in_)
 
-        def qk_transpose(name, vp):
-            words = (k_raw if name == "k" else q_raw)[:].bitcast(F32)
-            xps = ps_bank.tile([P, PACK, P], F32, tag="bank")
-            step = PACK * V // 2
-            for r in range(PACK):
-                first = r * (V // 2) + vp
-                nc.tensor.transpose(xps[:, r, :], words[:, first : first + step * (P - 1) + 1 : step], ident_hgc[:])
-            qk_ps[(name, vp)] = xps
+        def load_sc(pair, gu=None):
+            h, g = pair // 2, pair % 2
+            if pair not in sc_t:
+                sc_tile = sc_pool.tile([P, PACK, T], F32)
+                sc_t[pair] = sc_tile
+            src = sc[0, h, HALF * g : HALF * (g + 1), :].rearrange("(p j) u -> p j u", j=PACK)
+            us = slice(0, T) if gu is None else slice(HALF * gu, HALF * (gu + 1))
+            parts = 2 if gu is None else PIECES[2 * pair + gu]
+            for i in range(parts):
+                js = slice(PACK // parts * i, PACK // parts * (i + 1))
+                nc.sync.dma_start(out=sc_t[pair][:, js, us], in_=src[:, js, us])
 
-        def qk_copy(name, vp, engine):
-            if name not in qk_il:
-                tag = "k_il_q_out" if name == "k" else "k_raw_q_il"
-                xil = one.tile([P, H * NG * C, V // 2, 2 * PACK], BF16, tag=tag, align_bytes=64)
-                qk_il[name] = xil
+        def load_g(pair, gu=None):
+            h, g = pair // 2, pair % 2
+            if pair not in g_t:
+                g_tile = g_pool.tile([P, PACK, T], BF16)
+                g_t[pair] = g_tile
+            src = grad_out[0, h, HALF * g : HALF * (g + 1), :].rearrange("(p j) u -> p j u", j=PACK)
+            us = slice(0, T) if gu is None else slice(HALF * gu, HALF * (gu + 1))
+            nc.sync.dma_start(out=g_t[pair][:, :, us], in_=src[:, :, us])
+
+        def load_x(name):
+            tile, src = raw[name]
+            nc.sync.dma_start(out=tile[:], in_=src.rearrange("n h c (g u) v -> (n h c g) (u v)", g=NG))
+
+        def tanh(s):
+            th = th_pool.tile([P, PACK * HALF], F32)
+            th_t[s] = th
+            us = slice(HALF * (s % 2), HALF * (s % 2 + 1))
+            parts = PIECES.get(s, 1)
+            for i in range(parts):
+                js = slice(PACK // parts * i, PACK // parts * (i + 1))
+                nc.scalar.activation(
+                    th[:, piece(s, i)].rearrange("p (j u) -> p j u", u=HALF), sc_t[s // 2][:, js, us], ACT.Tanh, scale=1.0 / K
+                )
+
+        def slope(s):
+            th, h = th_t[s], s // 4
+            for i in range(PIECES.get(s, 1)):
+                cols = piece(s, i)
+                nc.vector.scalar_tensor_tensor(th[:, cols], th[:, cols], c_neg[:, h : h + 1], th[:, cols], ALU.mult, ALU.mult)
+
+        def dsc(s):
+            h, us = s // 4, slice(HALF * (s % 2), HALF * (s % 2 + 1))
+            d = d_pool.tile([P, PACK, HALF], BF16, align_bytes=64)
+            d_t[s] = d
+            nc.vector.scalar_tensor_tensor(
+                d[:],
+                th_t[s][:].rearrange("p (j u) -> p j u", j=PACK),
+                c_pos[:, h : h + 1],
+                g_t[s // 2][:, :, us],
+                ALU.add,
+                ALU.mult,
+            )
+            words = d[:].rearrange("p j u -> p (j u)").bitcast(F32)
+            row = HALF // 2
+            d_ps[s] = []
+            for b in range(PACK // 2):
+                bank = ps_d.tile([P, 2, 2, P], F32)
+                for jj in range(2):
+                    first = row * (2 * b + jj)
+                    for e in range(2):
+                        nc.tensor.transpose(bank[:, jj, e, :], words[:, first + e : first + row : 2], ident[:])
+                d_ps[s].append(bank)
+
+        def interleave(s):
+            h, g, gu = split(s)
+            if h == 0:
+                if (0, g) not in mix_t:
+                    mix = d_pool.tile([P, 2 * PACK, NG, P // 2, PACK], BF16, align_bytes=64)
+                    mix_t[(0, g)] = mix
+                for m0 in range(0, 2 * PACK, PACK):
+                    ms = slice(m0, m0 + PACK)
+                    nc.vector.tensor_copy(
+                        out=mix_t[(0, g)][:, ms, gu].rearrange("p m i j -> p i m j"),
+                        in_=d_t[s][:].rearrange("p j (i m) -> p i m j", m=2 * PACK)[:, :, ms, :],
+                    )
+            else:
+                mix = d_pool.tile([P, PACK, P, PACK], BF16, align_bytes=64)
+                mix_t[s] = mix
+                nc.vector.tensor_copy(
+                    out=mix[:].rearrange("p m i j -> p i m j"),
+                    in_=d_t[s][:].rearrange("p j (i m) -> p i m j", m=PACK),
+                )
+
+        def turn(s):
+            h, g, gu = split(s)
+            if h == 0:
+                if (0, gu) not in turned_t:
+                    turned = d_pool.tile([P, T * PACK], BF16, align_bytes=64)
+                    turned_t[(0, gu)] = turned
+                dst = turned_t[(0, gu)][:].bitcast(F32).rearrange("p (a j g i e) -> p a j g i e", a=2, j=PACK, g=NG, e=2)
+                for j in range(PACK):
+                    nc.scalar.copy(out=dst[:, :, j, g], in_=d_ps[s][j // 2][:, j % 2].rearrange("p e (i a) -> p a i e", a=2))
+            else:
+                turned = d_pool.tile([P, HALF * PACK], BF16, align_bytes=64)
+                turned_t[s] = turned
+                dst = turned[:].bitcast(F32).rearrange("p (b j i e) -> p b j i e", b=2, j=2, e=2)
+                for b in range(PACK // 2):
+                    nc.scalar.copy(out=dst[:, b], in_=d_ps[s][b][:].rearrange("p j e i -> p j i e"))
+
+        def quantise(pool, store, key, cols, in_):
+            if key not in store:
+                codes = pool.tile([P, T], U32, align_bytes=64)
+                scales = pool.tile([P, T], U8, align_bytes=64)
+                store[key] = (codes, scales)
+            nc.vector.quantize_mx(out=store[key][0][:, cols].bitcast(E5), scales=store[key][1][:, cols], in_=in_)
+
+        def quantise_t(h, n):
+            if h == 0:
+                quantise(t_code_pool, t_codes, (0, n), slice(0, T), mix_t[(0, n)][:].rearrange("p m g i j -> p (m g i j)"))
+            else:
+                g, gu = n // 2, n % 2
+                cols = slice(HALF * g, HALF * (g + 1))
+                quantise(t_code_pool, t_codes, (1, gu), cols, mix_t[4 + n][:].rearrange("p m i j -> p (m i j)"))
+
+        def quantise_u(h, n):
+            if h == 0:
+                quantise(u_code_pool, u_codes, (0, n), slice(0, T), turned_t[(0, n)][:])
+            else:
+                g, gu = n // 2, n % 2
+                quantise(u_code_pool, u_codes, (1, g), slice(HALF * gu, HALF * (gu + 1)), turned_t[4 + n][:])
+
+        def turn_x(name, pair, engine):
+            words = raw[name][0][:].bitcast(F32)
+            step = PACK * PAIRS
+            while len(x_ps.setdefault(name, [])) < min(PAIRS, pair + AHEAD + 1):
+                bank = ps_bank.tile([P, PACK, P], F32, tag="bank")
+                for r in range(PACK):
+                    first = PAIRS * r + len(x_ps[name])
+                    nc.tensor.transpose(bank[:, r, :], words[:, first : first + step * (P - 1) + 1 : step], ident_hgc[:])
+                x_ps[name].append(bank)
+            if name not in x_mix:
+                mix_x = one.tile([P, H * NG * C, PAIRS, 2 * PACK], BF16, tag=tag_b if name == "k" else tag_a, align_bytes=64)
+                x_mix[name] = mix_x
             copy_out(
                 engine,
-                qk_il[name][:, :, vp, :].rearrange("p x (e r) -> p x e r", e=2),
-                qk_ps[(name, vp)][:].bitcast(BF16).rearrange("p r (x e) -> p x e r", e=2),
+                x_mix[name][:, :, pair, :].rearrange("p x (e r) -> p x e r", e=2),
+                x_ps[name][pair][:].bitcast(BF16).rearrange("p r (x e) -> p x e r", e=2),
             )
 
-        def qk_quant(name, codes, scales, h):
-            flat = qk_il[name][:].rearrange("p x w e -> p (x w e)")
+        def quantise_x(name, h):
+            codes, scales = x_codes[name]
+            flat = x_mix[name][:].rearrange("p x v r -> p (x v r)")
             for i in range(NG * h, NG * (h + 1)):
-                nc.vector.quantize_mx(out=codes[:, i, :].bitcast(E4), scales=scales[:, i, :], in_=flat[:, 4 * K * i : 4 * K * (i + 1)])
-
-        st_t, mm_t = {}, {}
+                nc.vector.quantize_mx(out=codes[:, i, :].bitcast(E4), scales=scales[:, i, :], in_=flat[:, PACK * K * i : PACK * K * (i + 1)])
 
         def multiply(name, h, half, m, passes):
-            codes = tc_t if name == "Q" else dc_t
-            x_codes, x_scales = (k_codes, k_scales) if name == "Q" else (q_codes, q_scales)
-            if passes[0] == 0:
+            store = u_codes if name == "k" else t_codes
+            if 0 in passes:
                 mm = ps_bank.tile([P, K], F32, tag="bank")
                 mm_t[(name, h, half, m)] = mm
             for x in passes:
                 if h == 0:
-                    lhs, first = codes[(0, x)], P * (PACK * half + m)
+                    codes, scales = store[(0, x)]
+                    first = P * (PACK * half + m)
                 else:
-                    lhs, first = codes[(1, half)], HALF * x + P * m
+                    codes, scales = store[(1, half)]
+                    first = HALF * x + P * m
                 nc.tensor.matmul_mx(
                     out=mm_t[(name, h, half, m)][:],
-                    lhsT=lhs[0][:, first : first + P].bitcast(E5),
-                    lhsT_scale=lhs[1][:, first : first + P],
-                    rhs=x_codes[:, NG * h + x, :].bitcast(E4),
-                    rhs_scale=x_scales[:, NG * h + x, :],
+                    lhsT=codes[:, first : first + P].bitcast(E5),
+                    lhsT_scale=scales[:, first : first + P],
+                    rhs=x_codes[name][0][:, NG * h + x, :].bitcast(E4),
+                    rhs_scale=x_codes[name][1][:, NG * h + x, :],
                     start=(x == 0),
                     stop=(x == NG - 1),
                 )
 
-        def evacuate(name, h, half, m, engine):
+        def stage(name, h, half, m, engine, cs):
             key = (name, 0) if h == 0 else (name, 1, half)
             if key not in st_t:
                 if h == 0:
-                    st = one.tile([P, C, 2 * PACK, V], F32, tag="k_il_q_out" if name == "Q" else "q_raw_k_out", align_bytes=64)
+                    st = one.tile([P, C, 2 * PACK, V], F32, tag=tag_b if name == "k" else tag_c, align_bytes=64)
                 elif half == 0:
                     st = st_pool.tile([P, C, PACK, V], F32, align_bytes=64)
                 else:
-                    st = one.tile([P, C, PACK, V], F32, tag="k_il_q_out" if name == "Q" else "k_raw_q_il", align_bytes=64)
+                    st = one.tile([P, C, PACK, V], F32, tag=tag_b if name == "k" else tag_a, align_bytes=64)
                 st_t[key] = st
             row = PACK * half + m if h == 0 else m
-            copy_out(engine, st_t[key][:, :, row, :], mm_t[(name, h, half, m)][:].rearrange("p (c v) -> p c v", v=V))
+            copy_out(engine, st_t[key][:, cs, row, :], mm_t[(name, h, half, m)][:].rearrange("p (c v) -> p c v", v=V)[:, cs, :])
 
-        def store(name, h, part):
-            out = out_0 if name == "Q" else out_1
-            if h == 0:
-                cs = slice(C // 2 * part, C // 2 * (part + 1))
-                dst, src, runs = out[0, 0, cs], st_t[(name, 0)][:, cs], 2 * PACK
-            else:
-                dst, src, runs = out[0, 1, :, HALF * part : HALF * (part + 1), :], st_t[(name, 1, part)][:], PACK
-            nc.sync.dma_start(out=dst.rearrange("c (p m) v -> p c (m v)", m=runs), in_=src.rearrange("p c m v -> p c (m v)"))
+        def store_out(name, h, half, cs):
+            frames = slice(0, T) if h == 0 else slice(HALF * half, HALF * (half + 1))
+            key = (name, 0) if h == 0 else (name, 1, half)
+            out = out_0 if name == "k" else out_1
+            nc.sync.dma_start(
+                out=out[0, h, cs, frames, :].rearrange("c (p m) v -> p c (m v)", p=P),
+                in_=st_t[key][:, cs].rearrange("p c m v -> p c (m v)"),
+            )
+
+        halves_of_c = (slice(0, C // 2), slice(C // 2, C))
+
+        def open_groups(name, h, half):
+            for m in range(PACK):
+                multiply(name, h, half, m, [0])
+
+        def product(name, h, half, engines):
+            last = h == 1 and half == 1
+            for m in range(PACK):
+                multiply(name, h, half, m, [1] if (name, h, half, m) in mm_t else [0, 1])
+            for n, cs in enumerate(halves_of_c if last else (slice(0, C),)):
+                for m in range(PACK):
+                    stage(name, h, half, m, engines[PACK * n + m], cs)
+                if last:
+                    store_out(name, h, half, cs)
+            if h == 0 and half == 1:
+                for cs in halves_of_c:
+                    store_out(name, h, half, cs)
+            elif h == 1 and half == 0:
+                store_out(name, h, half, slice(0, C))
+
+        steps = {
+            "tanh": tanh,
+            "slope": slope,
+            "dsc": dsc,
+            "mix": interleave,
+            "turn": turn,
+            "qt": quantise_t,
+            "qu": quantise_u,
+            "turnx": turn_x,
+            "qx": quantise_x,
+            "open": open_groups,
+            "product": product,
+        }
+        loads = {"sc": load_sc, "g": load_g, "x": load_x}
+
+        def run(word, table):
+            fields = word.split(":")
+            table[fields[0]](*[int(a) if a in "01234567" else a for a in fields[1:]])
 
         ctx.enter_context(tc.manual_schedule())
-        for op in ORDER.split():
-            name, args = op[0], op[1:]
-            if name == "L":
-                if args == "k":
-                    load_qk(k_raw, k)
-                elif args == "q":
-                    load_qk(q_raw, q)
-                elif args[0] == "s":
-                    load_sc(int(args[2]), int(args[4]))
-                elif args in ("g00", "g01"):
-                    load_g(0, 0, int(args[2]))
-                else:
-                    load_g(int(args[1]) // 4, int(args[1]) // 2 % 2)
-            elif name in "kq" and args[0] == "x":
-                qk_transpose(name, int(args[1]))
-            elif name in "kq" and args[0] == "c":
-                qk_copy(name, int(args[1]), args[2])
-            elif name in "kq":
-                qk_quant(name, k_codes if name == "k" else q_codes, k_scales if name == "k" else q_scales, int(args[1]))
-            elif name == "T":
-                tanh(int(args[0]), int(args[2]))
-            elif name == "W":
-                slope(int(args[0]), int(args[2]))
-            elif name == "D":
-                dsc(int(args))
-            elif name == "I":
-                interleave(int(args))
-            elif name == "X":
-                transposes(int(args))
-            elif name == "C":
-                copy_t(int(args))
-            elif name == "A" and args[1:2] == "_":
-                quant_t0(int(args[2]))
-            elif name == "B" and args[1:2] == "_":
-                quant_u0(int(args[2]))
-            elif name == "A":
-                quant_t(int(args))
-            elif name == "B":
-                quant_u(int(args))
-            elif name == "N":
-                multiply(args[0], int(args[1]), int(args[2]), int(args[3]), [0])
-            elif name == "M":
-                multiply(args[0], int(args[1]), int(args[2]), int(args[3]), [1] if args[1:3] == "11" else [0, 1])
-            elif name == "E":
-                evacuate(args[0], int(args[1]), int(args[2]), int(args[3]), args[4])
-            elif name == "S":
-                store(args[2], int(args[1]), int(args[3]))
+        for word in LOADS.split():
+            run(word, loads)
+        for word in ORDER.split():
+            run(word, steps)

from contextlib import ExitStack

import concourse.mybir as mybir
from concourse.masks import make_identity

H, C, T, V = 2, 32, 1024, 16
P = 128
PACK = 4
HALF = P * PACK
NG = T // HALF
K = C * V
PAIRS = V // 2

FLOPS = 2 * 2 * H * T * T * K
BYTES = 2 * (2 * H * C * T * V) + 4 * H * T * T + 2 * H * T * T + 2 * (4 * H * C * T * V)

F32 = mybir.dt.float32
BF16 = mybir.dt.bfloat16
U32 = mybir.dt.uint32
U8 = mybir.dt.uint8
E4 = mybir.dt.float8_e4m3fn_x4
E5 = mybir.dt.float8_e5m2_x4
ALU = mybir.AluOpType
ACT = mybir.ActivationFunctionType

PIECES = {0: 4, 1: 2, 2: 2, 4: 2, 6: 2}

AHEAD = 2

LOADS = (
    "sc:0:0 g:0:0 sc:0:1 g:0:1 sc:1 x:k g:1 x:q sc:2 g:2 sc:3 g:3"
)

ORDER = (
    "tanh:0 slope:0 dsc:0 tanh:1 turn:0 slope:1 tanh:2 mix:0 dsc:1 slope:2 tanh:3 turn:1 mix:1 turnx:k:0:s "
    "turnx:k:1:s slope:3 turnx:k:2:s turnx:k:3:s qt:0:0 dsc:2 turnx:k:4:s turnx:k:5:s turnx:k:6:s turn:2 "
    "turnx:q:0:s dsc:3 mix:2 mix:3 turnx:k:7:v turnx:q:1:s turnx:q:2:s turn:3 qt:0:1 qx:k:1 turnx:q:3:s qx:k:0 "
    "tanh:4 turnx:q:4:s qu:0:0 qu:0:1 turnx:q:5:s turnx:q:6:v product:k:0:0:ssss product:k:0:1:ssss slope:4 "
    "turnx:q:7:v dsc:4 tanh:5 qx:q:0 mix:4 tanh:6 turn:4 qx:q:1 slope:5 product:q:0:0:ssss slope:6 "
    "product:q:0:1:ssss dsc:5 turn:5 dsc:6 tanh:7 qt:1:0 qu:1:0 qu:1:1 mix:6 product:k:1:0:ssss slope:7 qt:1:2 "
    "turn:6 product:q:1:0:ssss mix:5 dsc:7 qt:1:1 turn:7 mix:7 open:q:1:1 qt:1:3 qu:1:2 qu:1:3 "
    "product:q:1:1:vsvsvvss product:k:1:1:vvvvssss"
)


def tile_model_pa_v_kernel(tc, q, k, alphas, att1s, sc, grad_out, out_0, out_1):
    nc = tc.nc
    with ExitStack() as ctx:
        one = ctx.enter_context(tc.tile_pool(name="one", bufs=1))
        sc_pool = ctx.enter_context(tc.tile_pool(name="sc_pool", bufs=2))
        g_pool = ctx.enter_context(tc.tile_pool(name="g_pool", bufs=3))
        th_pool = ctx.enter_context(tc.tile_pool(name="th_pool", bufs=2))
        d_pool = ctx.enter_context(tc.tile_pool(name="d_pool", bufs=2))
        t_code_pool = ctx.enter_context(tc.tile_pool(name="t_code_pool", bufs=4))
        u_code_pool = ctx.enter_context(tc.tile_pool(name="u_code_pool", bufs=3))
        st_pool = ctx.enter_context(tc.tile_pool(name="st_pool", bufs=2))
        ps_d = ctx.enter_context(tc.psum_pool(name="ps_d", bufs=2))
        ps_bank = ctx.enter_context(tc.psum_pool(name="ps_bank", bufs=6))

        warm_in = one.tile([P, 1], F32)
        nc.gpsimd.memset(warm_in[:], 0.0)
        alpha_sb = one.tile([P, H], BF16)
        nc.sync.dma_start(out=alpha_sb[:], in_=alphas.rearrange("a h b c -> (a h b c)").partition_broadcast(P))
        warm_out = one.tile([P, 1], F32)
        nc.scalar.activation(warm_out[:], warm_in[:], ACT.Tanh)
        ident = one.tile([P, P], F32)
        make_identity(nc, ident[:])
        c_pos = one.tile([P, H], F32)
        c_neg = one.tile([P, H], F32)
        nc.gpsimd.tensor_scalar_mul(c_pos[:], alpha_sb[:], 1.0 / K)
        nc.gpsimd.tensor_scalar_mul(c_neg[:], alpha_sb[:], -1.0 / K)
        ident_hgc = one.tile([P, P], F32)
        for h in range(H):
            cols = slice(C * NG * h, C * NG * (h + 1))
            nc.vector.tensor_copy(
                out=ident_hgc[:, cols].rearrange("p (g c) -> p g c", g=NG),
                in_=ident[:, cols].rearrange("p (c g) -> p g c", g=NG),
            )

        tag_a, tag_b, tag_c = "k_raw_q_mix", "k_mix_q_out", "q_raw_k_out"
        raw = {}
        k_raw = one.tile([P, HALF * V], BF16, tag=tag_a, align_bytes=64)
        q_raw = one.tile([P, HALF * V], BF16, tag=tag_c, align_bytes=64)
        raw["k"], raw["q"] = (k_raw, k), (q_raw, q)
        x_codes = {}
        for name in "kq":
            codes = one.tile([P, H * NG, K], U32, name=name + "_codes", align_bytes=64)
            scales = one.tile([P, H * NG, K], U8, name=name + "_scales", align_bytes=64)
            x_codes[name] = (codes, scales)

        sc_t, g_t, th_t, d_t, d_ps, mix_t, turned_t = {}, {}, {}, {}, {}, {}, {}
        t_codes, u_codes, x_ps, x_mix, mm_t, st_t = {}, {}, {}, {}, {}, {}

        def split(s):
            return s // 4, (s // 2) % 2, s % 2

        def piece(s, i):
            width = PACK * HALF // PIECES.get(s, 1)
            return slice(width * i, width * (i + 1))

        def copy_out(engine, out, in_):
            if engine == "s":
                nc.scalar.copy(out=out, in_=in_)
            else:
                nc.vector.tensor_copy(out=out, in_=in_)

        def load_sc(pair, gu=None):
            h, g = pair // 2, pair % 2
            if pair not in sc_t:
                sc_tile = sc_pool.tile([P, PACK, T], F32)
                sc_t[pair] = sc_tile
            src = sc[0, h, HALF * g : HALF * (g + 1), :].rearrange("(p j) u -> p j u", j=PACK)
            us = slice(0, T) if gu is None else slice(HALF * gu, HALF * (gu + 1))
            parts = 2 if gu is None else PIECES[2 * pair + gu]
            for i in range(parts):
                js = slice(PACK // parts * i, PACK // parts * (i + 1))
                nc.sync.dma_start(out=sc_t[pair][:, js, us], in_=src[:, js, us])

        def load_g(pair, gu=None):
            h, g = pair // 2, pair % 2
            if pair not in g_t:
                g_tile = g_pool.tile([P, PACK, T], BF16)
                g_t[pair] = g_tile
            src = grad_out[0, h, HALF * g : HALF * (g + 1), :].rearrange("(p j) u -> p j u", j=PACK)
            us = slice(0, T) if gu is None else slice(HALF * gu, HALF * (gu + 1))
            nc.sync.dma_start(out=g_t[pair][:, :, us], in_=src[:, :, us])

        def load_x(name):
            tile, src = raw[name]
            nc.sync.dma_start(out=tile[:], in_=src.rearrange("n h c (g u) v -> (n h c g) (u v)", g=NG))

        def tanh(s):
            th = th_pool.tile([P, PACK * HALF], F32)
            th_t[s] = th
            us = slice(HALF * (s % 2), HALF * (s % 2 + 1))
            parts = PIECES.get(s, 1)
            for i in range(parts):
                js = slice(PACK // parts * i, PACK // parts * (i + 1))
                nc.scalar.activation(
                    th[:, piece(s, i)].rearrange("p (j u) -> p j u", u=HALF), sc_t[s // 2][:, js, us], ACT.Tanh, scale=1.0 / K
                )

        def slope(s):
            th, h = th_t[s], s // 4
            for i in range(PIECES.get(s, 1)):
                cols = piece(s, i)
                nc.vector.scalar_tensor_tensor(th[:, cols], th[:, cols], c_neg[:, h : h + 1], th[:, cols], ALU.mult, ALU.mult)

        def dsc(s):
            h, us = s // 4, slice(HALF * (s % 2), HALF * (s % 2 + 1))
            d = d_pool.tile([P, PACK, HALF], BF16, align_bytes=64)
            d_t[s] = d
            nc.vector.scalar_tensor_tensor(
                d[:],
                th_t[s][:].rearrange("p (j u) -> p j u", j=PACK),
                c_pos[:, h : h + 1],
                g_t[s // 2][:, :, us],
                ALU.add,
                ALU.mult,
            )
            words = d[:].rearrange("p j u -> p (j u)").bitcast(F32)
            row = HALF // 2
            d_ps[s] = []
            for b in range(PACK // 2):
                bank = ps_d.tile([P, 2, 2, P], F32)
                for jj in range(2):
                    first = row * (2 * b + jj)
                    for e in range(2):
                        nc.tensor.transpose(bank[:, jj, e, :], words[:, first + e : first + row : 2], ident[:])
                d_ps[s].append(bank)

        def interleave(s):
            h, g, gu = split(s)
            if h == 0:
                if (0, g) not in mix_t:
                    mix = d_pool.tile([P, 2 * PACK, NG, P // 2, PACK], BF16, align_bytes=64)
                    mix_t[(0, g)] = mix
                for m0 in range(0, 2 * PACK, PACK):
                    ms = slice(m0, m0 + PACK)
                    nc.vector.tensor_copy(
                        out=mix_t[(0, g)][:, ms, gu].rearrange("p m i j -> p i m j"),
                        in_=d_t[s][:].rearrange("p j (i m) -> p i m j", m=2 * PACK)[:, :, ms, :],
                    )
            else:
                mix = d_pool.tile([P, PACK, P, PACK], BF16, align_bytes=64)
                mix_t[s] = mix
                nc.vector.tensor_copy(
                    out=mix[:].rearrange("p m i j -> p i m j"),
                    in_=d_t[s][:].rearrange("p j (i m) -> p i m j", m=PACK),
                )

        def turn(s):
            h, g, gu = split(s)
            if h == 0:
                if (0, gu) not in turned_t:
                    turned = d_pool.tile([P, T * PACK], BF16, align_bytes=64)
                    turned_t[(0, gu)] = turned
                dst = turned_t[(0, gu)][:].bitcast(F32).rearrange("p (a j g i e) -> p a j g i e", a=2, j=PACK, g=NG, e=2)
                for j in range(PACK):
                    nc.scalar.copy(out=dst[:, :, j, g], in_=d_ps[s][j // 2][:, j % 2].rearrange("p e (i a) -> p a i e", a=2))
            else:
                turned = d_pool.tile([P, HALF * PACK], BF16, align_bytes=64)
                turned_t[s] = turned
                dst = turned[:].bitcast(F32).rearrange("p (b j i e) -> p b j i e", b=2, j=2, e=2)
                for b in range(PACK // 2):
                    nc.scalar.copy(out=dst[:, b], in_=d_ps[s][b][:].rearrange("p j e i -> p j i e"))

        def quantise(pool, store, key, cols, in_):
            if key not in store:
                codes = pool.tile([P, T], U32, align_bytes=64)
                scales = pool.tile([P, T], U8, align_bytes=64)
                store[key] = (codes, scales)
            nc.vector.quantize_mx(out=store[key][0][:, cols].bitcast(E5), scales=store[key][1][:, cols], in_=in_)

        def quantise_t(h, n):
            if h == 0:
                quantise(t_code_pool, t_codes, (0, n), slice(0, T), mix_t[(0, n)][:].rearrange("p m g i j -> p (m g i j)"))
            else:
                g, gu = n // 2, n % 2
                cols = slice(HALF * g, HALF * (g + 1))
                quantise(t_code_pool, t_codes, (1, gu), cols, mix_t[4 + n][:].rearrange("p m i j -> p (m i j)"))

        def quantise_u(h, n):
            if h == 0:
                quantise(u_code_pool, u_codes, (0, n), slice(0, T), turned_t[(0, n)][:])
            else:
                g, gu = n // 2, n % 2
                quantise(u_code_pool, u_codes, (1, g), slice(HALF * gu, HALF * (gu + 1)), turned_t[4 + n][:])

        def turn_x(name, pair, engine):
            words = raw[name][0][:].bitcast(F32)
            step = PACK * PAIRS
            while len(x_ps.setdefault(name, [])) < min(PAIRS, pair + AHEAD + 1):
                bank = ps_bank.tile([P, PACK, P], F32, tag="bank")
                for r in range(PACK):
                    first = PAIRS * r + len(x_ps[name])
                    nc.tensor.transpose(bank[:, r, :], words[:, first : first + step * (P - 1) + 1 : step], ident_hgc[:])
                x_ps[name].append(bank)
            if name not in x_mix:
                mix_x = one.tile([P, H * NG * C, PAIRS, 2 * PACK], BF16, tag=tag_b if name == "k" else tag_a, align_bytes=64)
                x_mix[name] = mix_x
            copy_out(
                engine,
                x_mix[name][:, :, pair, :].rearrange("p x (e r) -> p x e r", e=2),
                x_ps[name][pair][:].bitcast(BF16).rearrange("p r (x e) -> p x e r", e=2),
            )

        def quantise_x(name, h):
            codes, scales = x_codes[name]
            flat = x_mix[name][:].rearrange("p x v r -> p (x v r)")
            for i in range(NG * h, NG * (h + 1)):
                nc.vector.quantize_mx(out=codes[:, i, :].bitcast(E4), scales=scales[:, i, :], in_=flat[:, PACK * K * i : PACK * K * (i + 1)])

        def multiply(name, h, half, m, passes):
            store = u_codes if name == "k" else t_codes
            if 0 in passes:
                mm = ps_bank.tile([P, K], F32, tag="bank")
                mm_t[(name, h, half, m)] = mm
            for x in passes:
                if h == 0:
                    codes, scales = store[(0, x)]
                    first = P * (PACK * half + m)
                else:
                    codes, scales = store[(1, half)]
                    first = HALF * x + P * m
                nc.tensor.matmul_mx(
                    out=mm_t[(name, h, half, m)][:],
                    lhsT=codes[:, first : first + P].bitcast(E5),
                    lhsT_scale=scales[:, first : first + P],
                    rhs=x_codes[name][0][:, NG * h + x, :].bitcast(E4),
                    rhs_scale=x_codes[name][1][:, NG * h + x, :],
                    start=(x == 0),
                    stop=(x == NG - 1),
                )

        def stage(name, h, half, m, engine, cs):
            key = (name, 0) if h == 0 else (name, 1, half)
            if key not in st_t:
                if h == 0:
                    st = one.tile([P, C, 2 * PACK, V], F32, tag=tag_b if name == "k" else tag_c, align_bytes=64)
                elif half == 0:
                    st = st_pool.tile([P, C, PACK, V], F32, align_bytes=64)
                else:
                    st = one.tile([P, C, PACK, V], F32, tag=tag_b if name == "k" else tag_a, align_bytes=64)
                st_t[key] = st
            row = PACK * half + m if h == 0 else m
            copy_out(engine, st_t[key][:, cs, row, :], mm_t[(name, h, half, m)][:].rearrange("p (c v) -> p c v", v=V)[:, cs, :])

        def store_out(name, h, half, cs):
            frames = slice(0, T) if h == 0 else slice(HALF * half, HALF * (half + 1))
            key = (name, 0) if h == 0 else (name, 1, half)
            out = out_0 if name == "k" else out_1
            nc.sync.dma_start(
                out=out[0, h, cs, frames, :].rearrange("c (p m) v -> p c (m v)", p=P),
                in_=st_t[key][:, cs].rearrange("p c m v -> p c (m v)"),
            )

        halves_of_c = (slice(0, C // 2), slice(C // 2, C))

        def open_groups(name, h, half):
            for m in range(PACK):
                multiply(name, h, half, m, [0])

        def product(name, h, half, engines):
            last = h == 1 and half == 1
            for m in range(PACK):
                multiply(name, h, half, m, [1] if (name, h, half, m) in mm_t else [0, 1])
            for n, cs in enumerate(halves_of_c if last else (slice(0, C),)):
                for m in range(PACK):
                    stage(name, h, half, m, engines[PACK * n + m], cs)
                if last:
                    store_out(name, h, half, cs)
            if h == 0 and half == 1:
                for cs in halves_of_c:
                    store_out(name, h, half, cs)
            elif h == 1 and half == 0:
                store_out(name, h, half, slice(0, C))

        steps = {
            "tanh": tanh,
            "slope": slope,
            "dsc": dsc,
            "mix": interleave,
            "turn": turn,
            "qt": quantise_t,
            "qu": quantise_u,
            "turnx": turn_x,
            "qx": quantise_x,
            "open": open_groups,
            "product": product,
        }
        loads = {"sc": load_sc, "g": load_g, "x": load_x}

        def run(word, table):
            fields = word.split(":")
            table[fields[0]](*[int(a) if a in "01234567" else a for a in fields[1:]])

        ctx.enter_context(tc.manual_schedule())
        for word in LOADS.split():
            run(word, loads)
        for word in ORDER.split():
            run(word, steps)
